import numpy as np
import ml_dtypes


def mxq(x, axis, fmt="e4m3"):
    dtype, down = {"e4m3": (ml_dtypes.float8_e4m3fn, 7), "e5m2": (ml_dtypes.float8_e5m2, 14)}[fmt]
    v = np.moveaxis(np.asarray(x, np.float32).astype(ml_dtypes.bfloat16).astype(np.float64), axis, -1)
    blocks = v.reshape(v.shape[:-1] + (-1, 32))
    amax = np.abs(blocks).max(-1, keepdims=True)
    byte = np.maximum(np.where(amax > 0, np.frexp(amax)[1] - 1 + 127, 0) - down, 1)
    scale = np.exp2(byte - 127.0)
    codes = (blocks / scale).astype(np.float32).astype(dtype).astype(np.float64)
    return np.moveaxis((codes * scale).reshape(v.shape), -1, axis)


WIDE = False


def mx_kscale(k):
    if not WIDE:
        return np.ones(k)
    levels = np.array([10, -10, 5, -5, 0])
    if k % 512:
        return np.exp2(np.random.permutation(np.resize(levels, k // 32))).repeat(32)
    a = np.empty((k // 512, 16))
    for p in range(k // 512):
        a[p, :8] = np.random.permutation(np.resize(levels, 8))
        for g in range(8):
            far = levels[np.abs(levels - a[p, g]) >= 10]
            a[p, g + 8] = far[np.random.randint(len(far))]
    return np.exp2(a.ravel()).repeat(32)


BF16 = ml_dtypes.bfloat16


def bf(x):
    return np.asarray(x, np.float32).astype(BF16)


def f64(x):
    return np.asarray(x).astype(np.float64)


B, S, D, O = 2, 256, 2048, 4096

EPS = 1.0 / 137.0


def setup_inputs():
    s = mx_kscale(D)
    p = np.exp2(np.round(0.5 * np.log2(np.mean(1.0 / (s * s)))))
    q = np.exp2(np.round(0.5 * np.log2(np.mean(s * s))))
    return {"x": bf(np.random.standard_normal((B, S, D)) * 0.5 * s * p),
            "kernel": bf(np.random.standard_normal((D, O)) * 0.5 / s[:, None] * q),
            "bias": bf(np.random.standard_normal(O) * 0.1),
            "alpha": bf(1.0 + 0.1 * np.random.standard_normal(1))}


def core(x, kernel, bias, alpha):
    xf, kf = f64(x), f64(kernel)
    y = mxq(xf, 2, "e4m3") @ mxq(kf, 0, "e4m3")
    x_sq = np.sum(xf * xf, axis=-1, keepdims=True)
    k_sq = np.sum(kf * kf, axis=0, keepdims=True)
    distances = x_sq + k_sq - 2.0 * y
    y = (y * y) / (distances + EPS)
    y = y + f64(bias).reshape((1,) * (y.ndim - 1) + (-1,))
    scale = (np.sqrt(float(O)) / np.log1p(float(O))) ** f64(alpha)
    return y * scale


def e4m3fn_bytes(y):
    return np.clip(np.asarray(y, np.float64), -448.0, 448.0).astype(np.float32).astype(ml_dtypes.float8_e4m3fn).view(np.uint8)


Y_SCALE = 81.0


def reference(x, kernel, bias, alpha):
    out = core(x, kernel, bias, alpha)
    return out, e4m3fn_bytes(out * Y_SCALE)

@@ -1,0 +1,401 @@
+from contextlib import ExitStack
+import math
+
+import concourse.mybir as mybir
+from concourse.masks import make_identity
+
+F32 = mybir.dt.float32
+BF16 = mybir.dt.bfloat16
+U32 = mybir.dt.uint32
+U8 = mybir.dt.uint8
+FP8X4 = mybir.dt.float8_e4m3fn_x4
+FP8 = mybir.dt.float8_e4m3fn
+ACT = mybir.ActivationFunctionType
+ALU = mybir.AluOpType
+
+TOKENS, D, O = 512, 2048, 4096
+FLOPS = 2 * TOKENS * D * O
+
+P = 128
+PACK = 4
+K_PASS = P * PACK
+PASSES = D // K_PASS
+CHUNK = 512
+N_CHUNKS = O // CHUNK
+M_TILES = TOKENS // P
+BLOCKS = CHUNK // P
+N_BANKS = N_CHUNKS * M_TILES
+
+ROW_GROUPS = PASSES * PACK
+GRAM = 8
+GRAM_BLOCKS = 3
+SLOTS = 8
+LEAD = 6
+G_COLS = 208
+G_FIRST = 8
+LAST = N_BANKS - 2
+
+EPS = 1.0 / 137.0
+LOG_BASE = math.log(math.sqrt(float(O)) / math.log(float(O) + 1.0))
+Y_SCALE = 81.0
+
+
+def tile_yatnmn_kernel(tc, x, kernel, bias, alpha, out_0, out_1):
+    nc = tc.nc
+    xf = x.flatten_outer_dims()
+    o0f = out_0.flatten_outer_dims()
+    o1f = out_1.flatten_outer_dims()
+
+    with ExitStack() as ctx:
+        keep = ctx.enter_context(tc.tile_pool(name="keep", bufs=1))
+        work = ctx.enter_context(tc.tile_pool(name="work", bufs=2))
+        psum = ctx.enter_context(tc.psum_pool(name="psum", bufs=1))
+
+        raws = {}
+        groupeds = {}
+        kcodes = {}
+        kscales = {}
+        kparts = {}
+        grams = {}
+        ksqbs = {}
+        biases = {}
+        accs = {}
+        ts = {}
+        rss = {}
+        zps = {}
+        wps = {}
+        ops = {}
+        kcols = {}
+        xts = {}
+        gxs = {}
+
+        def new_raw(c):
+            raws[c] = work.tile([P, PASSES, PACK, CHUNK], BF16, name="raw", tag="raw", bufs=4)
+
+        def load_pass(c, g):
+            nc.sync.dma_start(
+                out=raws[c][:, g, :, :],
+                in_=kernel[g * K_PASS : (g + 1) * K_PASS, c * CHUNK : (c + 1) * CHUNK].rearrange(
+                    "(p j) w -> p j w", j=PACK
+                ),
+            )
+
+        def load(c):
+            new_raw(c)
+            for g in range(PASSES):
+                load_pass(c, g)
+
+        a_bf = keep.tile([P, 1], BF16, name="a_bf")
+        nc.sync.dma_start(out=a_bf[:], in_=alpha.partition_broadcast(P))
+        new_raw(0)
+        x_sb = []
+        for half in range(2):
+            load_pass(0, 2 * half)
+            load_pass(0, 2 * half + 1)
+            for m in (2 * half, 2 * half + 1):
+                xt_sb = keep.tile([P, D], BF16, name="x_sb%d" % m, tag="x_sb%d" % m)
+                nc.sync.dma_start(out=xt_sb[:], in_=xf[m * P : (m + 1) * P, :])
+                x_sb.append(xt_sb)
+        load(1)
+        load(2)
+        b_bf = keep.tile([P, O], BF16, name="b_bf")
+        nc.sync.dma_start(out=b_bf[:], in_=bias.partition_broadcast(P))
+
+        ident_bf = keep.tile([P, P], BF16, name="ident_bf")
+        make_identity(nc, ident_bf[:])
+        ident_f = keep.tile([P, P], F32, name="ident_f")
+        make_identity(nc, ident_f[:])
+
+        sqrt_s = keep.tile([P, 1], F32, name="sqrt_s")
+        nc.scalar.activation(out=sqrt_s[:], in_=a_bf[:], func=ACT.Exp, scale=0.5 * LOG_BASE)
+        s_col = keep.tile([P, 1], F32, name="s_col")
+        nc.scalar.activation(out=s_col[:], in_=a_bf[:], func=ACT.Exp, scale=LOG_BASE)
+        warm = keep.tile([P, 1], F32, name="warm")
+        nc.scalar.activation(out=warm[:], in_=s_col[:], func=ACT.Abs_reciprocal_sqrt)
+
+        xsq = keep.tile([P, M_TILES], F32, name="xsq")
+        cx = keep.tile([P, M_TILES], F32, name="cx")
+        xcodes = []
+        xscales = []
+
+        def x_front(m):
+            junk = work.tile([P, D], BF16, name="junk", tag="junk", bufs=2)
+            nc.scalar.activation(out=junk[:], in_=x_sb[m][:], func=ACT.Square, accum_out=xsq[:, m : m + 1])
+            xw = x_sb[m][:].bitcast(F32)
+            for h in range(2):
+                xt = psum.tile([P, 2, 2, P], F32, name="xt", tag="acc", bufs=4)
+                xts[(m, h)] = xt
+                for g2 in range(2):
+                    g = 2 * h + g2
+                    for u in range(2):
+                        nc.tensor.transpose(xt[:, g2, u, :], xw[:, 256 * g + u : 256 * (g + 1) : 2], ident_f[:])
+
+        def x_copy(m):
+            gx = work.tile([P, D], BF16, name="gx", tag="gx", bufs=2, align_bytes=64)
+            gxs[m] = gx
+            gxw = gx[:].bitcast(F32).rearrange("p (g r u) -> p g r u", g=PASSES, u=2)
+            for h in range(2):
+                nc.vector.tensor_copy(
+                    out=gxw[:, 2 * h : 2 * h + 2, :, :], in_=xts[(m, h)][:].rearrange("p g u r -> p g r u")
+                )
+
+        def x_quantize(m):
+            xc = keep.tile([P, PASSES * P], U32, name="xc%d" % m, tag="xc%d" % m, align_bytes=64)
+            xs = keep.tile([P, PASSES * P], U8, name="xs%d" % m, tag="xs%d" % m, align_bytes=64)
+            nc.vector.quantize_mx(out=xc[:].bitcast(FP8X4), scales=xs[:], in_=gxs[m][:])
+            xcodes.append(xc)
+            xscales.append(xs)
+
+        def g_cols(i):
+            if i >= G_FIRST:
+                return G_COLS
+            return 0
+
+        def new_grouped(i):
+            c, g = divmod(i, PASSES)
+            if g == 0:
+                kcodes[c] = work.tile([P, PASSES, CHUNK], U32, name="kc", tag="kc", bufs=3, align_bytes=64)
+                kscales[c] = work.tile([P, PASSES, CHUNK], U8, name="ks", tag="ks", bufs=3, align_bytes=64)
+            groupeds[i] = work.tile([P, 2, CHUNK, PACK], BF16, name="grouped", tag="grouped", bufs=2, align_bytes=64)
+
+        def interleave_g(i):
+            c, g = divmod(i, PASSES)
+            if g_cols(i) == 0:
+                return
+            new_grouped(i)
+            w0 = CHUNK - g_cols(i)
+            nc.gpsimd.tensor_scalar(
+                out=groupeds[i][:, :, w0:CHUNK, :],
+                in0=raws[c][:, g : g + 2, :, w0:CHUNK].rearrange("p a j w -> p a w j"),
+                scalar1=1.0,
+                scalar2=0.0,
+                op0=ALU.mult,
+                op1=ALU.add,
+            )
+
+        def interleave_v(i):
+            c, g = divmod(i, PASSES)
+            if g_cols(i) == 0:
+                new_grouped(i)
+            w0 = CHUNK - g_cols(i)
+            for a in range(2):
+                nc.vector.tensor_copy(
+                    out=groupeds[i][:, a, 0:w0, :].rearrange("p (c e) j -> p c j e", e=4),
+                    in_=raws[c][:, g + a, :, 0:w0].rearrange("p j (c e) -> p c j e", e=4),
+                )
+
+        def quantize(i):
+            c, g = divmod(i, PASSES)
+            nc.vector.quantize_mx(
+                out=kcodes[c][:, g : g + 2, :].rearrange("p a w -> p (a w)").bitcast(FP8X4),
+                scales=kscales[c][:, g : g + 2, :].rearrange("p a w -> p (a w)"),
+                in_=groupeds[i][:].rearrange("p a w j -> p (a w j)"),
+            )
+
+        def squares(i):
+            c, b = divmod(i, BLOCKS)
+            raw = raws[c]
+            cols = slice(b * P, (b + 1) * P)
+            if b == 0:
+                kparts[c] = work.tile([P, 2 * BLOCKS], F32, name="kpart", tag="kpart", bufs=2)
+                grams[c] = psum.tile([P, CHUNK], F32, name="gram", tag="gram", bufs=1)
+            first = GRAM if b > 0 else 0
+            for r in range(first):
+                g, j = divmod(r, PACK)
+                nc.tensor.matmul(
+                    out=grams[c][:, cols],
+                    lhsT=raw[:, g, j, cols],
+                    rhs=raw[:, g, j, cols],
+                    start=(r == 0),
+                    stop=(r == first - 1),
+                )
+            for h in range((ROW_GROUPS - first) // SLOTS):
+                tp = psum.tile([P, SLOTS * P], BF16, name="tp", tag="tp", bufs=3)
+                for s in range(SLOTS):
+                    g, j = divmod(first + SLOTS * h + s, PACK)
+                    nc.tensor.transpose(tp[:, s * P : (s + 1) * P], raw[:, g, j, cols], ident_bf[:])
+                junk = work.tile([P, D], BF16, name="junk", tag="junk", bufs=2)
+                nc.scalar.activation(
+                    out=junk[:, 0 : SLOTS * P],
+                    in_=tp[:],
+                    func=ACT.Square,
+                    accum_out=kparts[c][:, 2 * b + h : 2 * b + h + 1],
+                )
+
+        def diagonal(i):
+            c, b = divmod(i, BLOCKS)
+            if b == 0:
+                return
+            junkf = work.tile([P, P], F32, name="junkf", tag="junkf", bufs=2)
+            nc.vector.scalar_tensor_tensor(
+                out=junkf[:],
+                in0=grams[c][:, b * P : (b + 1) * P],
+                scalar=1.0,
+                in1=ident_f[:],
+                op0=ALU.mult,
+                op1=ALU.mult,
+                accum_out=kparts[c][:, 2 * b + 1 : 2 * b + 2],
+            )
+
+        def sum_ksq(c):
+            kcol = work.tile([P, BLOCKS], F32, name="kcol", tag="kcol", bufs=2)
+            nc.vector.tensor_reduce(
+                out=kcol[:], in_=kparts[c][:].rearrange("p (b h) -> p b h", h=2), axis=mybir.AxisListType.X, op=ALU.add
+            )
+            kcols[c] = kcol
+
+        def spread_ksq(c):
+            kb = psum.tile([P, CHUNK], F32, name="kb", tag="tp", bufs=3)
+            for b in range(BLOCKS):
+                nc.tensor.transpose(
+                    kb[:, b * P : (b + 1) * P], kcols[c][:, b : b + 1].to_broadcast([P, P]), ident_f[:]
+                )
+            ksqb = work.tile([P, CHUNK], F32, name="ksqb", tag="ksqb", bufs=3)
+            nc.scalar.copy(out=ksqb[:], in_=kb[:])
+            ksqbs[c] = ksqb
+
+        def mx(n):
+            c, m = divmod(n, M_TILES)
+            acc = psum.tile([P, CHUNK], F32, name="acc", tag="acc", bufs=4)
+            accs[n] = acc
+            for g in range(PASSES):
+                nc.tensor.matmul_mx(
+                    out=acc[:],
+                    lhsT=xcodes[m][:, g * P : (g + 1) * P].bitcast(FP8X4),
+                    lhsT_scale=xscales[m][:, g * P : (g + 1) * P],
+                    rhs=kcodes[c][:, g, :].bitcast(FP8X4),
+                    rhs_scale=kscales[c][:, g, :],
+                    start=(g == 0),
+                    stop=(g == PASSES - 1),
+                )
+
+        def dist(n):
+            c, m = divmod(n, M_TILES)
+            t = work.tile([P, CHUNK], F32, name="t", tag="t", bufs=4)
+            nc.vector.scalar_tensor_tensor(
+                out=t[:], in0=accs[n][:], scalar=-2.0, in1=ksqbs[c][:], op0=ALU.mult, op1=ALU.add
+            )
+            ts[n] = t
+
+        def rsqrt(n):
+            c, m = divmod(n, M_TILES)
+            rs = work.tile([P, CHUNK], F32, name="rs", tag="rs", bufs=4)
+            nc.scalar.activation(
+                out=rs[:], in_=ts[n][:], func=ACT.Abs_reciprocal_sqrt, bias=cx[:, m : m + 1], scale=1.0
+            )
+            rss[n] = rs
+
+        def ratio(n):
+            if n % 2 == 0:
+                zps[n] = work.tile([P, 2, CHUNK], F32, name="zp", tag="zp", bufs=3)
+            nc.vector.tensor_tensor(out=zps[n - n % 2][:, n % 2, :], in0=accs[n][:], in1=rss[n][:], op=ALU.mult)
+
+        def square2(n):
+            wp = work.tile([P, 2, CHUNK], F32, name="wp", tag="wp", bufs=3)
+            wps[n] = wp
+            if n == LAST:
+                for a in range(2):
+                    nc.scalar.activation(out=wp[:, a, :], in_=zps[n][:, a, :], func=ACT.Square, scale=sqrt_s[:, 0:1])
+            else:
+                nc.scalar.activation(out=wp[:], in_=zps[n][:], func=ACT.Square, scale=sqrt_s[:, 0:1])
+
+        def finish_v(n):
+            c, m = divmod(n, M_TILES)
+            op = work.tile([P, 2, CHUNK], F32, name="op", tag="op", bufs=3)
+            ops[n] = op
+            cols = slice(c * CHUNK, (c + 1) * CHUNK)
+            if n == LAST:
+                o1 = work.tile([P, 2, CHUNK], FP8, name="o1", tag="o1", bufs=3)
+                for a in range(2):
+                    rows = slice((m + a) * P, (m + a + 1) * P)
+                    nc.vector.scalar_tensor_tensor(
+                        out=op[:, a, :],
+                        in0=b_bf[:, cols],
+                        scalar=s_col[:, 0:1],
+                        in1=wps[n][:, a, :],
+                        op0=ALU.mult,
+                        op1=ALU.add,
+                    )
+                    nc.sync.dma_start(out=o0f[rows, cols], in_=op[:, a, :])
+                for a in range(2):
+                    rows = slice((m + a) * P, (m + a + 1) * P)
+                    nc.vector.tensor_scalar(
+                        out=o1[:, a, :], in0=op[:, a, :], scalar1=Y_SCALE, scalar2=None, op0=ALU.mult, saturate=False
+                    )
+                    nc.sync.dma_start(out=o1f[rows, cols], in_=o1[:, a, :].bitcast(U8))
+                return
+            nc.vector.scalar_tensor_tensor(
+                out=op[:],
+                in0=b_bf[:, cols].unsqueeze(1).to_broadcast([P, 2, CHUNK]),
+                scalar=s_col[:, 0:1],
+                in1=wps[n][:],
+                op0=ALU.mult,
+                op1=ALU.add,
+            )
+            nc.sync.dma_start(out=o0f[m * P : (m + 2) * P, cols].rearrange("(a p) w -> p a w", a=2), in_=op[:])
+
+        def finish_s(n):
+            c, m = divmod(n, M_TILES)
+            if n == LAST:
+                return
+            o1 = work.tile([P, 2, CHUNK], FP8, name="o1", tag="o1", bufs=3)
+            nc.scalar.activation(out=o1[:], in_=ops[n][:], func=ACT.Copy, scale=Y_SCALE, saturate=False)
+            nc.sync.dma_start(
+                out=o1f[m * P : (m + 2) * P, c * CHUNK : (c + 1) * CHUNK].rearrange("(a p) w -> p a w", a=2),
+                in_=o1[:].bitcast(U8),
+            )
+
+        def valid(n):
+            return 0 <= n < N_BANKS
+
+        with tc.manual_schedule(engines={mybir.EngineType.DVE, mybir.EngineType.Pool}):
+            for k in range(-(LEAD // 2), N_BANKS // 2 + 4):
+                n0 = 2 * k
+                i0 = n0 + LEAD
+                if valid(i0 - 3) and (i0 - 3) % PASSES == PASSES - 1:
+                    spread_ksq((i0 - 3) // PASSES)
+                for n in (n0 - 2, n0 - 1):
+                    if valid(n):
+                        rsqrt(n)
+                if valid(n0 - 4):
+                    square2(n0 - 4)
+                if valid(n0 - 8):
+                    finish_s(n0 - 8)
+                if i0 == 0 or i0 == 2:
+                    x_front(i0)
+                    x_front(i0 + 1)
+                if valid(i0):
+                    if i0 % PASSES == 0 and 3 <= i0 // PASSES + 2 < N_CHUNKS:
+                        load(i0 // PASSES + 2)
+                    squares(i0)
+                    squares(i0 + 1)
+                if valid(i0):
+                    interleave_v(i0)
+                if valid(n0 - 6):
+                    finish_v(n0 - 6)
+                if i0 == 2 or i0 == 4:
+                    x_quantize(i0 - 2)
+                    x_quantize(i0 - 1)
+                if i0 == 4:
+                    nc.vector.tensor_scalar(out=cx[:], in0=xsq[:], scalar1=EPS, scalar2=None, op0=ALU.add)
+                if valid(i0 - 2):
+                    quantize(i0 - 2)
+                if valid(i0 + 2):
+                    interleave_g(i0 + 2)
+                if i0 == 0 or i0 == 2:
+                    x_copy(i0)
+                    x_copy(i0 + 1)
+                for n in (n0 - 2, n0 - 1):
+                    if valid(n):
+                        ratio(n)
+                for n in (n0 + 2, n0 + 3):
+                    if valid(n):
+                        mx(n)
+                for i in (i0 - 2, i0 - 1):
+                    if valid(i):
+                        diagonal(i)
+                for n in (n0, n0 + 1):
+                    if valid(n):
+                        dist(n)
+                if valid(i0 - 1) and (i0 - 1) % PASSES == PASSES - 1:
+                    sum_ksq((i0 - 1) // PASSES)

@@ -31,7 +31,7 @@ GRAM = 8
 GRAM_BLOCKS = 3
 SLOTS = 8
 LEAD = 6
-G_COLS = 208
+G_COLS = 256
 G_FIRST = 8
 LAST = N_BANKS - 2
 
@@ -371,8 +371,6 @@ def tile_yatnmn_kernel(tc, x, kernel, bias, alpha, out_0, out_1):
                     squares(i0 + 1)
                 if valid(i0):
                     interleave_v(i0)
-                if valid(n0 - 6):
-                    finish_v(n0 - 6)
                 if i0 == 2 or i0 == 4:
                     x_quantize(i0 - 2)
                     x_quantize(i0 - 1)
@@ -382,6 +380,8 @@ def tile_yatnmn_kernel(tc, x, kernel, bias, alpha, out_0, out_1):
                     quantize(i0 - 2)
                 if valid(i0 + 2):
                     interleave_g(i0 + 2)
+                if valid(n0 - 6):
+                    finish_v(n0 - 6)
                 if i0 == 0 or i0 == 2:
                     x_copy(i0)
                     x_copy(i0 + 1)

@@ -34,6 +34,7 @@ LEAD = 6
 G_COLS = 256
 G_FIRST = 8
 LAST = N_BANKS - 2
+CAST_EVERY = 4
 
 EPS = 1.0 / 137.0
 LOG_BASE = math.log(math.sqrt(float(O)) / math.log(float(O) + 1.0))
@@ -147,8 +148,12 @@ def tile_yatnmn_kernel(tc, x, kernel, bias, alpha, out_0, out_1):
             xscales.append(xs)
 
         def g_cols(i):
-            if i >= G_FIRST:
+            if i >= G_FIRST + 6:
                 return G_COLS
+            if i >= G_FIRST + 2:
+                return 208
+            if i >= G_FIRST:
+                return 96
             return 0
 
         def new_grouped(i):
@@ -334,12 +339,17 @@ def tile_yatnmn_kernel(tc, x, kernel, bias, alpha, out_0, out_1):
             )
             nc.sync.dma_start(out=o0f[m * P : (m + 2) * P, cols].rearrange("(a p) w -> p a w", a=2), in_=op[:])
 
-        def finish_s(n):
+        def finish_s(n, on_vector):
             c, m = divmod(n, M_TILES)
-            if n == LAST:
+            if n == LAST or ((n // 2) % CAST_EVERY == CAST_EVERY - 1) != on_vector:
                 return
             o1 = work.tile([P, 2, CHUNK], FP8, name="o1", tag="o1", bufs=3)
-            nc.scalar.activation(out=o1[:], in_=ops[n][:], func=ACT.Copy, scale=Y_SCALE, saturate=False)
+            if on_vector:
+                nc.vector.tensor_scalar(
+                    out=o1[:], in0=ops[n][:], scalar1=Y_SCALE, scalar2=None, op0=ALU.mult, saturate=False
+                )
+            else:
+                nc.scalar.activation(out=o1[:], in_=ops[n][:], func=ACT.Copy, scale=Y_SCALE, saturate=False)
             nc.sync.dma_start(
                 out=o1f[m * P : (m + 2) * P, c * CHUNK : (c + 1) * CHUNK].rearrange("(a p) w -> p a w", a=2),
                 in_=o1[:].bitcast(U8),
@@ -360,7 +370,7 @@ def tile_yatnmn_kernel(tc, x, kernel, bias, alpha, out_0, out_1):
                 if valid(n0 - 4):
                     square2(n0 - 4)
                 if valid(n0 - 8):
-                    finish_s(n0 - 8)
+                    finish_s(n0 - 8, False)
                 if i0 == 0 or i0 == 2:
                     x_front(i0)
                     x_front(i0 + 1)
@@ -380,6 +390,8 @@ def tile_yatnmn_kernel(tc, x, kernel, bias, alpha, out_0, out_1):
                     quantize(i0 - 2)
                 if valid(i0 + 2):
                     interleave_g(i0 + 2)
+                if valid(n0 - 8):
+                    finish_s(n0 - 8, True)
                 if valid(n0 - 6):
                     finish_v(n0 - 6)
                 if i0 == 0 or i0 == 2:

@@ -185,8 +185,8 @@ def tile_yatnmn_kernel(tc, x, kernel, bias, alpha, out_0, out_1):
             w0 = CHUNK - g_cols(i)
             for a in range(2):
                 nc.vector.tensor_copy(
-                    out=groupeds[i][:, a, 0:w0, :].rearrange("p (c e) j -> p c j e", e=4),
-                    in_=raws[c][:, g + a, :, 0:w0].rearrange("p j (c e) -> p c j e", e=4),
+                    out=groupeds[i][:, a, 0:w0, :].rearrange("p (c e) j -> p c j e", e=8),
+                    in_=raws[c][:, g + a, :, 0:w0].rearrange("p j (c e) -> p c j e", e=8),
                 )
 
         def quantize(i):

from contextlib import ExitStack
import math

import concourse.mybir as mybir
from concourse.masks import make_identity

F32 = mybir.dt.float32
BF16 = mybir.dt.bfloat16
U32 = mybir.dt.uint32
U8 = mybir.dt.uint8
FP8X4 = mybir.dt.float8_e4m3fn_x4
FP8 = mybir.dt.float8_e4m3fn
ACT = mybir.ActivationFunctionType
ALU = mybir.AluOpType

TOKENS, D, O = 512, 2048, 4096
FLOPS = 2 * TOKENS * D * O

P = 128
PACK = 4
K_PASS = P * PACK
PASSES = D // K_PASS
CHUNK = 512
N_CHUNKS = O // CHUNK
M_TILES = TOKENS // P
BLOCKS = CHUNK // P
N_BANKS = N_CHUNKS * M_TILES

ROW_GROUPS = PASSES * PACK
GRAM = 8
GRAM_BLOCKS = 3
SLOTS = 8
LEAD = 6
G_COLS = 256
G_FIRST = 8
LAST = N_BANKS - 2
CAST_EVERY = 4

EPS = 1.0 / 137.0
LOG_BASE = math.log(math.sqrt(float(O)) / math.log(float(O) + 1.0))
Y_SCALE = 81.0


def tile_yatnmn_kernel(tc, x, kernel, bias, alpha, out_0, out_1):
    nc = tc.nc
    xf = x.flatten_outer_dims()
    o0f = out_0.flatten_outer_dims()
    o1f = out_1.flatten_outer_dims()

    with ExitStack() as ctx:
        keep = ctx.enter_context(tc.tile_pool(name="keep", bufs=1))
        work = ctx.enter_context(tc.tile_pool(name="work", bufs=2))
        psum = ctx.enter_context(tc.psum_pool(name="psum", bufs=1))

        raws = {}
        groupeds = {}
        kcodes = {}
        kscales = {}
        kparts = {}
        grams = {}
        ksqbs = {}
        biases = {}
        accs = {}
        ts = {}
        rss = {}
        zps = {}
        wps = {}
        ops = {}
        kcols = {}
        xts = {}
        gxs = {}

        def new_raw(c):
            raws[c] = work.tile([P, PASSES, PACK, CHUNK], BF16, name="raw", tag="raw", bufs=4)

        def load_pass(c, g):
            nc.sync.dma_start(
                out=raws[c][:, g, :, :],
                in_=kernel[g * K_PASS : (g + 1) * K_PASS, c * CHUNK : (c + 1) * CHUNK].rearrange(
                    "(p j) w -> p j w", j=PACK
                ),
            )

        def load(c):
            new_raw(c)
            for g in range(PASSES):
                load_pass(c, g)

        a_bf = keep.tile([P, 1], BF16, name="a_bf")
        nc.sync.dma_start(out=a_bf[:], in_=alpha.partition_broadcast(P))
        new_raw(0)
        x_sb = []
        for half in range(2):
            load_pass(0, 2 * half)
            load_pass(0, 2 * half + 1)
            for m in (2 * half, 2 * half + 1):
                xt_sb = keep.tile([P, D], BF16, name="x_sb%d" % m, tag="x_sb%d" % m)
                nc.sync.dma_start(out=xt_sb[:], in_=xf[m * P : (m + 1) * P, :])
                x_sb.append(xt_sb)
        load(1)
        load(2)
        b_bf = keep.tile([P, O], BF16, name="b_bf")
        nc.sync.dma_start(out=b_bf[:], in_=bias.partition_broadcast(P))

        ident_bf = keep.tile([P, P], BF16, name="ident_bf")
        make_identity(nc, ident_bf[:])
        ident_f = keep.tile([P, P], F32, name="ident_f")
        make_identity(nc, ident_f[:])

        sqrt_s = keep.tile([P, 1], F32, name="sqrt_s")
        nc.scalar.activation(out=sqrt_s[:], in_=a_bf[:], func=ACT.Exp, scale=0.5 * LOG_BASE)
        s_col = keep.tile([P, 1], F32, name="s_col")
        nc.scalar.activation(out=s_col[:], in_=a_bf[:], func=ACT.Exp, scale=LOG_BASE)
        warm = keep.tile([P, 1], F32, name="warm")
        nc.scalar.activation(out=warm[:], in_=s_col[:], func=ACT.Abs_reciprocal_sqrt)

        xsq = keep.tile([P, M_TILES], F32, name="xsq")
        cx = keep.tile([P, M_TILES], F32, name="cx")
        xcodes = []
        xscales = []

        def x_front(m):
            junk = work.tile([P, D], BF16, name="junk", tag="junk", bufs=2)
            nc.scalar.activation(out=junk[:], in_=x_sb[m][:], func=ACT.Square, accum_out=xsq[:, m : m + 1])
            xw = x_sb[m][:].bitcast(F32)
            for h in range(2):
                xt = psum.tile([P, 2, 2, P], F32, name="xt", tag="acc", bufs=4)
                xts[(m, h)] = xt
                for g2 in range(2):
                    g = 2 * h + g2
                    for u in range(2):
                        nc.tensor.transpose(xt[:, g2, u, :], xw[:, 256 * g + u : 256 * (g + 1) : 2], ident_f[:])

        def x_copy(m):
            gx = work.tile([P, D], BF16, name="gx", tag="gx", bufs=2, align_bytes=64)
            gxs[m] = gx
            gxw = gx[:].bitcast(F32).rearrange("p (g r u) -> p g r u", g=PASSES, u=2)
            for h in range(2):
                nc.vector.tensor_copy(
                    out=gxw[:, 2 * h : 2 * h + 2, :, :], in_=xts[(m, h)][:].rearrange("p g u r -> p g r u")
                )

        def x_quantize(m):
            xc = keep.tile([P, PASSES * P], U32, name="xc%d" % m, tag="xc%d" % m, align_bytes=64)
            xs = keep.tile([P, PASSES * P], U8, name="xs%d" % m, tag="xs%d" % m, align_bytes=64)
            nc.vector.quantize_mx(out=xc[:].bitcast(FP8X4), scales=xs[:], in_=gxs[m][:])
            xcodes.append(xc)
            xscales.append(xs)

        def g_cols(i):
            if i >= G_FIRST + 6:
                return G_COLS
            if i >= G_FIRST + 2:
                return 208
            if i >= G_FIRST:
                return 96
            return 0

        def new_grouped(i):
            c, g = divmod(i, PASSES)
            if g == 0:
                kcodes[c] = work.tile([P, PASSES, CHUNK], U32, name="kc", tag="kc", bufs=3, align_bytes=64)
                kscales[c] = work.tile([P, PASSES, CHUNK], U8, name="ks", tag="ks", bufs=3, align_bytes=64)
            groupeds[i] = work.tile([P, 2, CHUNK, PACK], BF16, name="grouped", tag="grouped", bufs=2, align_bytes=64)

        def interleave_g(i):
            c, g = divmod(i, PASSES)
            if g_cols(i) == 0:
                return
            new_grouped(i)
            w0 = CHUNK - g_cols(i)
            nc.gpsimd.tensor_scalar(
                out=groupeds[i][:, :, w0:CHUNK, :],
                in0=raws[c][:, g : g + 2, :, w0:CHUNK].rearrange("p a j w -> p a w j"),
                scalar1=1.0,
                scalar2=0.0,
                op0=ALU.mult,
                op1=ALU.add,
            )

        def interleave_v(i):
            c, g = divmod(i, PASSES)
            if g_cols(i) == 0:
                new_grouped(i)
            w0 = CHUNK - g_cols(i)
            for a in range(2):
                nc.vector.tensor_copy(
                    out=groupeds[i][:, a, 0:w0, :].rearrange("p (c e) j -> p c j e", e=8),
                    in_=raws[c][:, g + a, :, 0:w0].rearrange("p j (c e) -> p c j e", e=8),
                )

        def quantize(i):
            c, g = divmod(i, PASSES)
            nc.vector.quantize_mx(
                out=kcodes[c][:, g : g + 2, :].rearrange("p a w -> p (a w)").bitcast(FP8X4),
                scales=kscales[c][:, g : g + 2, :].rearrange("p a w -> p (a w)"),
                in_=groupeds[i][:].rearrange("p a w j -> p (a w j)"),
            )

        def squares(i):
            c, b = divmod(i, BLOCKS)
            raw = raws[c]
            cols = slice(b * P, (b + 1) * P)
            if b == 0:
                kparts[c] = work.tile([P, 2 * BLOCKS], F32, name="kpart", tag="kpart", bufs=2)
                grams[c] = psum.tile([P, CHUNK], F32, name="gram", tag="gram", bufs=1)
            first = GRAM if b > 0 else 0
            for r in range(first):
                g, j = divmod(r, PACK)
                nc.tensor.matmul(
                    out=grams[c][:, cols],
                    lhsT=raw[:, g, j, cols],
                    rhs=raw[:, g, j, cols],
                    start=(r == 0),
                    stop=(r == first - 1),
                )
            for h in range((ROW_GROUPS - first) // SLOTS):
                tp = psum.tile([P, SLOTS * P], BF16, name="tp", tag="tp", bufs=3)
                for s in range(SLOTS):
                    g, j = divmod(first + SLOTS * h + s, PACK)
                    nc.tensor.transpose(tp[:, s * P : (s + 1) * P], raw[:, g, j, cols], ident_bf[:])
                junk = work.tile([P, D], BF16, name="junk", tag="junk", bufs=2)
                nc.scalar.activation(
                    out=junk[:, 0 : SLOTS * P],
                    in_=tp[:],
                    func=ACT.Square,
                    accum_out=kparts[c][:, 2 * b + h : 2 * b + h + 1],
                )

        def diagonal(i):
            c, b = divmod(i, BLOCKS)
            if b == 0:
                return
            junkf = work.tile([P, P], F32, name="junkf", tag="junkf", bufs=2)
            nc.vector.scalar_tensor_tensor(
                out=junkf[:],
                in0=grams[c][:, b * P : (b + 1) * P],
                scalar=1.0,
                in1=ident_f[:],
                op0=ALU.mult,
                op1=ALU.mult,
                accum_out=kparts[c][:, 2 * b + 1 : 2 * b + 2],
            )

        def sum_ksq(c):
            kcol = work.tile([P, BLOCKS], F32, name="kcol", tag="kcol", bufs=2)
            nc.vector.tensor_reduce(
                out=kcol[:], in_=kparts[c][:].rearrange("p (b h) -> p b h", h=2), axis=mybir.AxisListType.X, op=ALU.add
            )
            kcols[c] = kcol

        def spread_ksq(c):
            kb = psum.tile([P, CHUNK], F32, name="kb", tag="tp", bufs=3)
            for b in range(BLOCKS):
                nc.tensor.transpose(
                    kb[:, b * P : (b + 1) * P], kcols[c][:, b : b + 1].to_broadcast([P, P]), ident_f[:]
                )
            ksqb = work.tile([P, CHUNK], F32, name="ksqb", tag="ksqb", bufs=3)
            nc.scalar.copy(out=ksqb[:], in_=kb[:])
            ksqbs[c] = ksqb

        def mx(n):
            c, m = divmod(n, M_TILES)
            acc = psum.tile([P, CHUNK], F32, name="acc", tag="acc", bufs=4)
            accs[n] = acc
            for g in range(PASSES):
                nc.tensor.matmul_mx(
                    out=acc[:],
                    lhsT=xcodes[m][:, g * P : (g + 1) * P].bitcast(FP8X4),
                    lhsT_scale=xscales[m][:, g * P : (g + 1) * P],
                    rhs=kcodes[c][:, g, :].bitcast(FP8X4),
                    rhs_scale=kscales[c][:, g, :],
                    start=(g == 0),
                    stop=(g == PASSES - 1),
                )

        def dist(n):
            c, m = divmod(n, M_TILES)
            t = work.tile([P, CHUNK], F32, name="t", tag="t", bufs=4)
            nc.vector.scalar_tensor_tensor(
                out=t[:], in0=accs[n][:], scalar=-2.0, in1=ksqbs[c][:], op0=ALU.mult, op1=ALU.add
            )
            ts[n] = t

        def rsqrt(n):
            c, m = divmod(n, M_TILES)
            rs = work.tile([P, CHUNK], F32, name="rs", tag="rs", bufs=4)
            nc.scalar.activation(
                out=rs[:], in_=ts[n][:], func=ACT.Abs_reciprocal_sqrt, bias=cx[:, m : m + 1], scale=1.0
            )
            rss[n] = rs

        def ratio(n):
            if n % 2 == 0:
                zps[n] = work.tile([P, 2, CHUNK], F32, name="zp", tag="zp", bufs=3)
            nc.vector.tensor_tensor(out=zps[n - n % 2][:, n % 2, :], in0=accs[n][:], in1=rss[n][:], op=ALU.mult)

        def square2(n):
            wp = work.tile([P, 2, CHUNK], F32, name="wp", tag="wp", bufs=3)
            wps[n] = wp
            if n == LAST:
                for a in range(2):
                    nc.scalar.activation(out=wp[:, a, :], in_=zps[n][:, a, :], func=ACT.Square, scale=sqrt_s[:, 0:1])
            else:
                nc.scalar.activation(out=wp[:], in_=zps[n][:], func=ACT.Square, scale=sqrt_s[:, 0:1])

        def finish_v(n):
            c, m = divmod(n, M_TILES)
            op = work.tile([P, 2, CHUNK], F32, name="op", tag="op", bufs=3)
            ops[n] = op
            cols = slice(c * CHUNK, (c + 1) * CHUNK)
            if n == LAST:
                o1 = work.tile([P, 2, CHUNK], FP8, name="o1", tag="o1", bufs=3)
                for a in range(2):
                    rows = slice((m + a) * P, (m + a + 1) * P)
                    nc.vector.scalar_tensor_tensor(
                        out=op[:, a, :],
                        in0=b_bf[:, cols],
                        scalar=s_col[:, 0:1],
                        in1=wps[n][:, a, :],
                        op0=ALU.mult,
                        op1=ALU.add,
                    )
                    nc.sync.dma_start(out=o0f[rows, cols], in_=op[:, a, :])
                for a in range(2):
                    rows = slice((m + a) * P, (m + a + 1) * P)
                    nc.vector.tensor_scalar(
                        out=o1[:, a, :], in0=op[:, a, :], scalar1=Y_SCALE, scalar2=None, op0=ALU.mult, saturate=False
                    )
                    nc.sync.dma_start(out=o1f[rows, cols], in_=o1[:, a, :].bitcast(U8))
                return
            nc.vector.scalar_tensor_tensor(
                out=op[:],
                in0=b_bf[:, cols].unsqueeze(1).to_broadcast([P, 2, CHUNK]),
                scalar=s_col[:, 0:1],
                in1=wps[n][:],
                op0=ALU.mult,
                op1=ALU.add,
            )
            nc.sync.dma_start(out=o0f[m * P : (m + 2) * P, cols].rearrange("(a p) w -> p a w", a=2), in_=op[:])

        def finish_s(n, on_vector):
            c, m = divmod(n, M_TILES)
            if n == LAST or ((n // 2) % CAST_EVERY == CAST_EVERY - 1) != on_vector:
                return
            o1 = work.tile([P, 2, CHUNK], FP8, name="o1", tag="o1", bufs=3)
            if on_vector:
                nc.vector.tensor_scalar(
                    out=o1[:], in0=ops[n][:], scalar1=Y_SCALE, scalar2=None, op0=ALU.mult, saturate=False
                )
            else:
                nc.scalar.activation(out=o1[:], in_=ops[n][:], func=ACT.Copy, scale=Y_SCALE, saturate=False)
            nc.sync.dma_start(
                out=o1f[m * P : (m + 2) * P, c * CHUNK : (c + 1) * CHUNK].rearrange("(a p) w -> p a w", a=2),
                in_=o1[:].bitcast(U8),
            )

        def valid(n):
            return 0 <= n < N_BANKS

        with tc.manual_schedule(engines={mybir.EngineType.DVE, mybir.EngineType.Pool}):
            for k in range(-(LEAD // 2), N_BANKS // 2 + 4):
                n0 = 2 * k
                i0 = n0 + LEAD
                if valid(i0 - 3) and (i0 - 3) % PASSES == PASSES - 1:
                    spread_ksq((i0 - 3) // PASSES)
                for n in (n0 - 2, n0 - 1):
                    if valid(n):
                        rsqrt(n)
                if valid(n0 - 4):
                    square2(n0 - 4)
                if valid(n0 - 8):
                    finish_s(n0 - 8, False)
                if i0 == 0 or i0 == 2:
                    x_front(i0)
                    x_front(i0 + 1)
                if valid(i0):
                    if i0 % PASSES == 0 and 3 <= i0 // PASSES + 2 < N_CHUNKS:
                        load(i0 // PASSES + 2)
                    squares(i0)
                    squares(i0 + 1)
                if valid(i0):
                    interleave_v(i0)
                if i0 == 2 or i0 == 4:
                    x_quantize(i0 - 2)
                    x_quantize(i0 - 1)
                if i0 == 4:
                    nc.vector.tensor_scalar(out=cx[:], in0=xsq[:], scalar1=EPS, scalar2=None, op0=ALU.add)
                if valid(i0 - 2):
                    quantize(i0 - 2)
                if valid(i0 + 2):
                    interleave_g(i0 + 2)
                if valid(n0 - 8):
                    finish_s(n0 - 8, True)
                if valid(n0 - 6):
                    finish_v(n0 - 6)
                if i0 == 0 or i0 == 2:
                    x_copy(i0)
                    x_copy(i0 + 1)
                for n in (n0 - 2, n0 - 1):
                    if valid(n):
                        ratio(n)
                for n in (n0 + 2, n0 + 3):
                    if valid(n):
                        mx(n)
                for i in (i0 - 2, i0 - 1):
                    if valid(i):
                        diagonal(i)
                for n in (n0, n0 + 1):
                    if valid(n):
                        dist(n)
                if valid(i0 - 1) and (i0 - 1) % PASSES == PASSES - 1:
                    sum_ksq((i0 - 1) // PASSES)
